import numpy as np
import ml_dtypes


BF16 = ml_dtypes.bfloat16


def bf(x):
    return np.asarray(x, np.float32).astype(BF16)


def f64(x):
    return np.asarray(x).astype(np.float64)


E2M1 = np.array([0.0, 0.5, 1.0, 1.5, 2.0, 3.0, 4.0, 6.0, -0.0, -0.5, -1.0, -1.5, -2.0, -3.0, -4.0, -6.0])


def pack_weight(w, fmt):
    k, n = w.shape
    w = f64(bf(w)).reshape(k // 32, 32, n)
    amax = np.abs(w).max(1)
    if fmt == "e4m3":
        byte = np.frexp(amax)[1] - 1 + 127 - 7
    else:
        mant, ex = np.frexp(amax / 6.0)
        byte = np.where(mant > 0.5, ex, ex - 1) + 127
    byte = np.clip(np.where(amax > 0, byte, 1), 1, 254)
    scaled = (w * np.exp2(127.0 - byte)[:, None, :]).reshape(k, n).astype(np.float32)
    by_word = np.ascontiguousarray(scaled.reshape(k // 512, 128, 4, n).transpose(0, 1, 3, 2))
    if fmt == "e4m3":
        words = by_word.astype(ml_dtypes.float8_e4m3fn).view(np.uint8)
    else:
        c = by_word.astype(ml_dtypes.float4_e2m1fn).view(np.uint8) & 0xF
        words = c[..., 0::2] | (c[..., 1::2] << 4)
    return np.ascontiguousarray(words), np.ascontiguousarray(byte.astype(np.uint8).reshape(k // 512, 16, n))


def unpack_weight(words, scales, fmt):
    g, p, n, _ = words.shape
    if fmt == "e4m3":
        vals = np.ascontiguousarray(words).view(ml_dtypes.float8_e4m3fn).astype(np.float64)
    else:
        nib = np.empty((g, p, n, 4), np.uint8)
        nib[..., 0::2] = words & 0xF
        nib[..., 1::2] = words >> 4
        vals = E2M1[nib]
    vals = vals * np.repeat(np.exp2(scales.astype(np.float64) - 127.0), 8, axis=1)[..., None]
    return vals.transpose(0, 1, 3, 2).reshape(g * 512, n)

def pack4(w):
    words, scales = pack_weight(w, "e2m1")
    return words.reshape(words.shape[0], 128, -1), scales


def unpack4(words, scales):
    return unpack_weight(words.reshape(words.shape[0], 128, -1, 2), scales, "e2m1")


def kspread(k):
    return np.exp2(np.repeat(np.random.randint(-6, 7, k // 32), 32).astype(np.float64))


B, T, C, R, H, DN, DR, DV = 2, 256, 2048, 512, 16, 128, 64, 128
DQ = DN + DR
NF = DR // 2


def rotate_half(u):
    u1, u2 = u[..., : u.shape[-1] // 2], u[..., u.shape[-1] // 2 :]
    return np.concatenate([-u2, u1], axis=-1)


def setup_inputs():
    s = kspread(C)
    x = np.random.standard_normal((B, T, C)) * s
    x_words, x_scales = pack4(x.reshape(B * T, C).T)
    freqs_cis = bf(np.stack([np.random.uniform(size=(T, NF)), np.random.uniform(size=(T, NF))], axis=-1))
    words, scales = pack4(np.random.standard_normal((C, H * DQ)) / np.sqrt(C) / s[:, None])
    return {
        "x_words": x_words,
        "x_scales": x_scales,
        "freqs_cis": freqs_cis,
        "w_q_words": words,
        "w_q_scales": scales,
    }


def reference(x_words, x_scales, freqs_cis, w_q_words, w_q_scales):
    q = (unpack4(x_words, x_scales).T.reshape(B, T, C) @ unpack4(w_q_words, w_q_scales)).reshape(B, T, H, DQ)
    q_nope, q_rope = q[..., :DN], q[..., DN:]
    freqs = f64(freqs_cis)
    cos = freqs[..., 0][None, :, None, :]
    sin = freqs[..., 1][None, :, None, :]
    rep = DR // cos.shape[-1]
    cos = np.tile(cos, (1, 1, 1, rep))
    sin = np.tile(sin, (1, 1, 1, rep))
    q_rope = q_rope * cos + rotate_half(q_rope) * sin
    return np.concatenate([q_nope, q_rope], axis=-1)

@@ -1,0 +1,213 @@
+from contextlib import ExitStack
+
+import concourse.mybir as mybir
+
+TOKENS, K, COLS = 512, 2048, 3072
+FLOPS = 2 * TOKENS * K * COLS
+
+F32 = mybir.dt.float32
+BF16 = mybir.dt.bfloat16
+I32 = mybir.dt.int32
+U8 = mybir.dt.uint8
+FP4X4 = mybir.dt.float4_e2m1fn_x4
+MULT = mybir.AluOpType.mult
+ADD = mybir.AluOpType.add
+
+P = 128
+PASSES = K // 512
+TILES = TOKENS // P
+BLOCK = 512
+UNIT = 64
+HALF = 32
+
+CHUNKS = ((0, 512), (512, 1024), (2048, 1024), (1536, 512))
+BLOCK_ORDER = (0, 1, 2, 4, 5, 3)
+WARM = 7
+
+
+def tile_fa3mlaattention_pb_kernel(tc, x_words, x_scales, freqs_cis, w_q_words, w_q_scales, out):
+    nc = tc.nc
+    rows = out.rearrange("b t h d -> (b t) (h d)")
+
+    with ExitStack() as ctx:
+        keep = ctx.enter_context(tc.tile_pool(name="keep", bufs=1))
+        prods = ctx.enter_context(tc.tile_pool(name="prods", bufs=3))
+        results = ctx.enter_context(tc.tile_pool(name="results", bufs=24))
+        psum = ctx.enter_context(tc.psum_pool(name="psum", bufs=8))
+        ctx.enter_context(tc.manual_schedule())
+
+        zeros = keep.tile([P, BLOCK], BF16, name="zeros")
+        table_load = keep.tile([P, 1], BF16, name="table_load")
+        freqs = keep.tile([P, 2, HALF, 2], BF16, name="freqs")
+        table = keep.tile([P, 2, 4, HALF], F32, name="table")
+        x_codes = keep.tile([P, PASSES, 2 * TOKENS], U8, name="x_codes", align_bytes=64)
+        x_planes = keep.tile([P, PASSES, TOKENS], U8, name="x_planes", align_bytes=64)
+        w_codes = []
+        w_planes = []
+        for c in range(len(CHUNKS)):
+            width = CHUNKS[c][1]
+            w_codes.append(keep.tile([P, PASSES, 2 * width], U8, name="w_codes%d" % c, align_bytes=64))
+            w_planes.append(keep.tile([P, PASSES, width], U8, name="w_planes%d" % c, align_bytes=64))
+
+        def load_x_codes(g0, g1):
+            nc.sync.dma_start(
+                out=x_codes[:, g0:g1, :].bitcast(I32),
+                in_=x_words[g0:g1, :, :].rearrange("g p c -> p g c").bitcast(I32),
+            )
+
+        def load_w_codes(c, g0, g1):
+            start, width = CHUNKS[c]
+            nc.sync.dma_start(
+                out=w_codes[c][:, g0:g1, :].bitcast(I32),
+                in_=w_q_words[g0:g1, :, 2 * start : 2 * (start + width)].rearrange("g p c -> p g c").bitcast(I32),
+            )
+
+        def load_scales(plane, scales):
+            for q in range(4):
+                nc.sync.dma_start(
+                    out=plane[32 * q : 32 * q + 4, :, :].bitcast(I32),
+                    in_=scales[:, 4 * q : 4 * q + 4, :].rearrange("g r n -> r g n").bitcast(I32),
+                )
+
+        def w_scale_cols(c):
+            start, width = CHUNKS[c]
+            return w_q_scales[:, :, start : start + width]
+
+        nc.gpsimd.memset(zeros[:], 0.0)
+        nc.vector.memset(x_planes[:].rearrange("p g n -> p (g n)").bitcast(I32), 0)
+        for c in range(len(CHUNKS)):
+            nc.vector.memset(w_planes[c][:].rearrange("p g n -> p (g n)").bitcast(I32), 0)
+
+        load_x_codes(0, 1)
+        load_w_codes(0, 0, 1)
+        load_scales(x_planes, x_scales)
+        load_scales(w_planes[0], w_scale_cols(0))
+        load_w_codes(0, 1, 2)
+        load_x_codes(1, 2)
+        load_w_codes(0, 2, 4)
+        load_x_codes(2, 4)
+        load_scales(w_planes[1], w_scale_cols(1))
+        load_w_codes(1, 0, 2)
+        load_w_codes(1, 2, 4)
+        load_scales(w_planes[2], w_scale_cols(2))
+        load_w_codes(2, 0, 2)
+        load_w_codes(2, 2, 4)
+        load_scales(w_planes[3], w_scale_cols(3))
+        load_w_codes(3, 0, 4)
+
+        nc.gpsimd.dma_start(out=freqs[:], in_=freqs_cis.rearrange("(t p) j e -> p t j e", p=P))
+        nc.scalar.copy(out=table_load[:], in_=zeros[:, 0:1])
+        nc.gpsimd.tensor_copy(out=table[:, :, 0, :], in_=freqs[:, :, :, 0])
+        nc.gpsimd.tensor_copy(out=table[:, :, 3, :], in_=freqs[:, :, :, 0])
+        nc.gpsimd.tensor_copy(out=table[:, :, 2, :], in_=freqs[:, :, :, 1])
+        nc.gpsimd.tensor_scalar(out=table[:, :, 1, :], in0=freqs[:, :, :, 1], scalar1=-1.0, scalar2=None, op0=MULT)
+
+        warm = psum.tile([P, BLOCK], F32, name="acc")
+        for i in range(WARM):
+            nc.tensor.matmul(warm[:], lhsT=zeros[:, 0:P], rhs=zeros[:], start=True, stop=True)
+
+        def chunk_of(block):
+            for c in range(len(CHUNKS)):
+                start, width = CHUNKS[c]
+                if start <= block * BLOCK < start + width:
+                    return c, block * BLOCK - start
+            raise ValueError("block")
+
+        def mx_pass(acc, m, block, g, first, width):
+            c, at = chunk_of(block)
+            a = at + first
+            nc.tensor.matmul_mx(
+                out=acc,
+                lhsT=x_codes[:, g, 2 * P * m : 2 * P * (m + 1)].bitcast(FP4X4),
+                lhsT_scale=x_planes[:, g, P * m : P * (m + 1)],
+                rhs=w_codes[c][:, g, 2 * a : 2 * (a + width)].bitcast(FP4X4),
+                rhs_scale=w_planes[c][:, g, a : a + width],
+                start=(g == 0),
+                stop=(g == PASSES - 1),
+            )
+
+        def rope_products(acc3, rope, m):
+            n = len(range(rope, acc3.shape[1], 3))
+            prod = prods.tile([P, 2, 3, 2, HALF], F32, name="prod")
+            r = acc3[:, rope::3, :].rearrange("p r (h j) -> p r h j", h=2)
+            t = table[:, m % 2, :, :].rearrange("p (c h) j -> p c h j", h=2)
+            nc.vector.tensor_tensor(
+                out=prod[:, :, 0:n, :, :].rearrange("p h r c j -> p r c h j"),
+                in0=r.unsqueeze(2).to_broadcast([P, n, 2, 2, HALF]),
+                in1=t.unsqueeze(1).to_broadcast([P, n, 2, 2, HALF]),
+                op=MULT,
+            )
+            return prod, n
+
+        def plain_copies(acc3, res3, rope):
+            for r in range(3):
+                if r != rope:
+                    nc.scalar.copy(out=res3[:, r::3, :], in_=acc3[:, r::3, :])
+
+        def rope_sum(res3, rope, prod, n):
+            nc.vector.tensor_tensor(
+                out=res3[:, rope::3, :],
+                in0=prod[:, 0, 0:n, :, :].rearrange("p r c j -> p r (c j)"),
+                in1=prod[:, 1, 0:n, :, :].rearrange("p r c j -> p r (c j)"),
+                op=ADD,
+            )
+
+        def store(res, m, block, first, width):
+            col = block * BLOCK + first
+            nc.sync.dma_start(out=rows[P * m : P * (m + 1), col : col + width], in_=res[:, first : first + width])
+
+        def units(tile_2d):
+            return tile_2d.rearrange("p (u w) -> p u w", w=UNIT)
+
+        waiting = []
+
+        def finish():
+            if waiting:
+                res, m, block, rope, prod, n = waiting[0]
+                rope_sum(units(res[:]), rope, prod, n)
+                store(res, m, block, 0, BLOCK)
+                waiting.clear()
+
+        def epilogue(acc, m, block):
+            rope = (2 - 2 * block) % 3
+            res = results.tile([P, BLOCK], F32, name="res")
+            prod, n = rope_products(units(acc[:]), rope, m)
+            plain_copies(units(acc[:]), units(res[:]), rope)
+            finish()
+            waiting.append((res, m, block, rope, prod, n))
+
+        accs = []
+        for m in range(TILES):
+            acc = psum.tile([P, BLOCK], F32, name="acc")
+            accs.append(acc)
+        for g in range(PASSES):
+            for m in range(TILES):
+                mx_pass(accs[m][:], m, BLOCK_ORDER[0], g, 0, BLOCK)
+        for m in range(TILES):
+            epilogue(accs[m], m, BLOCK_ORDER[0])
+
+        for block in BLOCK_ORDER[1:]:
+            for m in range(TILES):
+                if block == BLOCK_ORDER[-1] and m == TILES - 1:
+                    continue
+                acc = psum.tile([P, BLOCK], F32, name="acc")
+                for g in range(PASSES):
+                    mx_pass(acc[:], m, block, g, 0, BLOCK)
+                epilogue(acc, m, block)
+
+        m, block = TILES - 1, BLOCK_ORDER[-1]
+        res = results.tile([P, BLOCK], F32, name="res")
+        acc_a = psum.tile([P, BLOCK], F32, name="acc")
+        acc_b = psum.tile([P, BLOCK], F32, name="acc")
+        acc_c = psum.tile([P, BLOCK], F32, name="acc")
+        for acc, first, width in ((acc_a, 128, 256), (acc_b, 384, 128), (acc_c, 0, 128)):
+            for g in range(PASSES):
+                mx_pass(acc[:, 0:width], m, block, g, first, width)
+        prod, n = rope_products(units(acc_a[:, 0:256]), 0, m)
+        plain_copies(units(acc_a[:, 0:256]), units(res[:, 128:384]), 0)
+        finish()
+        rope_sum(units(res[:, 128:384]), 0, prod, n)
+        nc.scalar.copy(out=res[:, 384:512], in_=acc_b[:, 0:128])
+        store(res, m, block, 128, 384)
+        nc.vector.tensor_copy(out=res[:, 0:128], in_=acc_c[:, 0:128])
+        store(res, m, block, 0, 128)

@@ -20,7 +20,7 @@ BLOCK = 512
 UNIT = 64
 HALF = 32
 
-CHUNKS = ((0, 512), (512, 1024), (2048, 1024), (1536, 512))
+CHUNKS = ((0, 512), (512, 512), (1024, 512), (2048, 1024), (1536, 512))
 BLOCK_ORDER = (0, 1, 2, 4, 5, 3)
 WARM = 7
 
@@ -65,8 +65,8 @@ def tile_fa3mlaattention_pb_kernel(tc, x_words, x_scales, freqs_cis, w_q_words, 
         def load_scales(plane, scales):
             for q in range(4):
                 nc.sync.dma_start(
-                    out=plane[32 * q : 32 * q + 4, :, :].bitcast(I32),
-                    in_=scales[:, 4 * q : 4 * q + 4, :].rearrange("g r n -> r g n").bitcast(I32),
+                    out=plane[q : P : 32, :, :].bitcast(I32),
+                    in_=scales[:, q : 16 : 4, :].rearrange("g r n -> r g n").bitcast(I32),
                 )
 
         def w_scale_cols(c):
@@ -86,14 +86,9 @@ def tile_fa3mlaattention_pb_kernel(tc, x_words, x_scales, freqs_cis, w_q_words, 
         load_x_codes(1, 2)
         load_w_codes(0, 2, 4)
         load_x_codes(2, 4)
-        load_scales(w_planes[1], w_scale_cols(1))
-        load_w_codes(1, 0, 2)
-        load_w_codes(1, 2, 4)
-        load_scales(w_planes[2], w_scale_cols(2))
-        load_w_codes(2, 0, 2)
-        load_w_codes(2, 2, 4)
-        load_scales(w_planes[3], w_scale_cols(3))
-        load_w_codes(3, 0, 4)
+        for c in range(1, len(CHUNKS)):
+            load_scales(w_planes[c], w_scale_cols(c))
+            load_w_codes(c, 0, 4)
 
         nc.gpsimd.dma_start(out=freqs[:], in_=freqs_cis.rearrange("(t p) j e -> p t j e", p=P))
         nc.scalar.copy(out=table_load[:], in_=zeros[:, 0:1])

@@ -86,11 +86,11 @@ def tile_fa3mlaattention_pb_kernel(tc, x_words, x_scales, freqs_cis, w_q_words, 
         load_x_codes(1, 2)
         load_w_codes(0, 2, 4)
         load_x_codes(2, 4)
+        nc.sync.dma_start(out=freqs[:], in_=freqs_cis.rearrange("(t p) j e -> p t j e", p=P))
         for c in range(1, len(CHUNKS)):
             load_scales(w_planes[c], w_scale_cols(c))
             load_w_codes(c, 0, 4)
 
-        nc.gpsimd.dma_start(out=freqs[:], in_=freqs_cis.rearrange("(t p) j e -> p t j e", p=P))
         nc.scalar.copy(out=table_load[:], in_=zeros[:, 0:1])
         nc.gpsimd.tensor_copy(out=table[:, :, 0, :], in_=freqs[:, :, :, 0])
         nc.gpsimd.tensor_copy(out=table[:, :, 3, :], in_=freqs[:, :, :, 0])
@@ -166,9 +166,9 @@ def tile_fa3mlaattention_pb_kernel(tc, x_words, x_scales, freqs_cis, w_q_words, 
         def epilogue(acc, m, block):
             rope = (2 - 2 * block) % 3
             res = results.tile([P, BLOCK], F32, name="res")
-            prod, n = rope_products(units(acc[:]), rope, m)
-            plain_copies(units(acc[:]), units(res[:]), rope)
+            nc.scalar.copy(out=res[:], in_=acc[:])
             finish()
+            prod, n = rope_products(units(res[:]), rope, m)
             waiting.append((res, m, block, rope, prod, n))
 
         accs = []

@@ -163,6 +163,14 @@ def tile_fa3mlaattention_pb_kernel(tc, x_words, x_scales, freqs_cis, w_q_words, 
                 store(res, m, block, 0, BLOCK)
                 waiting.clear()
 
+        def direct_epilogue(acc, m, block):
+            rope = (2 - 2 * block) % 3
+            res = results.tile([P, BLOCK], F32, name="res")
+            prod, n = rope_products(units(acc[:]), rope, m)
+            plain_copies(units(acc[:]), units(res[:]), rope)
+            finish()
+            waiting.append((res, m, block, rope, prod, n))
+
         def epilogue(acc, m, block):
             rope = (2 - 2 * block) % 3
             res = results.tile([P, BLOCK], F32, name="res")
@@ -188,7 +196,10 @@ def tile_fa3mlaattention_pb_kernel(tc, x_words, x_scales, freqs_cis, w_q_words, 
                 acc = psum.tile([P, BLOCK], F32, name="acc")
                 for g in range(PASSES):
                     mx_pass(acc[:], m, block, g, 0, BLOCK)
-                epilogue(acc, m, block)
+                if block == BLOCK_ORDER[-1]:
+                    direct_epilogue(acc, m, block)
+                else:
+                    epilogue(acc, m, block)
 
         m, block = TILES - 1, BLOCK_ORDER[-1]
         res = results.tile([P, BLOCK], F32, name="res")
@@ -199,9 +210,9 @@ def tile_fa3mlaattention_pb_kernel(tc, x_words, x_scales, freqs_cis, w_q_words, 
             for g in range(PASSES):
                 mx_pass(acc[:, 0:width], m, block, g, first, width)
         prod, n = rope_products(units(acc_a[:, 0:256]), 0, m)
-        plain_copies(units(acc_a[:, 0:256]), units(res[:, 128:384]), 0)
         finish()
         rope_sum(units(res[:, 128:384]), 0, prod, n)
+        nc.scalar.copy(out=res[:, 192:320], in_=acc_a[:, 64:192])
         nc.scalar.copy(out=res[:, 384:512], in_=acc_b[:, 0:128])
         store(res, m, block, 128, 384)
         nc.vector.tensor_copy(out=res[:, 0:128], in_=acc_c[:, 0:128])

from contextlib import ExitStack

import concourse.mybir as mybir

TOKENS, K, COLS = 512, 2048, 3072
FLOPS = 2 * TOKENS * K * COLS

F32 = mybir.dt.float32
BF16 = mybir.dt.bfloat16
I32 = mybir.dt.int32
U8 = mybir.dt.uint8
FP4X4 = mybir.dt.float4_e2m1fn_x4
MULT = mybir.AluOpType.mult
ADD = mybir.AluOpType.add

P = 128
PASSES = K // 512
TILES = TOKENS // P
BLOCK = 512
UNIT = 64
HALF = 32

CHUNKS = ((0, 512), (512, 512), (1024, 512), (2048, 1024), (1536, 512))
BLOCK_ORDER = (0, 1, 2, 4, 5, 3)
WARM = 7


def tile_fa3mlaattention_pb_kernel(tc, x_words, x_scales, freqs_cis, w_q_words, w_q_scales, out):
    nc = tc.nc
    rows = out.rearrange("b t h d -> (b t) (h d)")

    with ExitStack() as ctx:
        keep = ctx.enter_context(tc.tile_pool(name="keep", bufs=1))
        prods = ctx.enter_context(tc.tile_pool(name="prods", bufs=3))
        results = ctx.enter_context(tc.tile_pool(name="results", bufs=24))
        psum = ctx.enter_context(tc.psum_pool(name="psum", bufs=8))
        ctx.enter_context(tc.manual_schedule())

        zeros = keep.tile([P, BLOCK], BF16, name="zeros")
        table_load = keep.tile([P, 1], BF16, name="table_load")
        freqs = keep.tile([P, 2, HALF, 2], BF16, name="freqs")
        table = keep.tile([P, 2, 4, HALF], F32, name="table")
        x_codes = keep.tile([P, PASSES, 2 * TOKENS], U8, name="x_codes", align_bytes=64)
        x_planes = keep.tile([P, PASSES, TOKENS], U8, name="x_planes", align_bytes=64)
        w_codes = []
        w_planes = []
        for c in range(len(CHUNKS)):
            width = CHUNKS[c][1]
            w_codes.append(keep.tile([P, PASSES, 2 * width], U8, name="w_codes%d" % c, align_bytes=64))
            w_planes.append(keep.tile([P, PASSES, width], U8, name="w_planes%d" % c, align_bytes=64))

        def load_x_codes(g0, g1):
            nc.sync.dma_start(
                out=x_codes[:, g0:g1, :].bitcast(I32),
                in_=x_words[g0:g1, :, :].rearrange("g p c -> p g c").bitcast(I32),
            )

        def load_w_codes(c, g0, g1):
            start, width = CHUNKS[c]
            nc.sync.dma_start(
                out=w_codes[c][:, g0:g1, :].bitcast(I32),
                in_=w_q_words[g0:g1, :, 2 * start : 2 * (start + width)].rearrange("g p c -> p g c").bitcast(I32),
            )

        def load_scales(plane, scales):
            for q in range(4):
                nc.sync.dma_start(
                    out=plane[q : P : 32, :, :].bitcast(I32),
                    in_=scales[:, q : 16 : 4, :].rearrange("g r n -> r g n").bitcast(I32),
                )

        def w_scale_cols(c):
            start, width = CHUNKS[c]
            return w_q_scales[:, :, start : start + width]

        nc.gpsimd.memset(zeros[:], 0.0)
        nc.vector.memset(x_planes[:].rearrange("p g n -> p (g n)").bitcast(I32), 0)
        for c in range(len(CHUNKS)):
            nc.vector.memset(w_planes[c][:].rearrange("p g n -> p (g n)").bitcast(I32), 0)

        load_x_codes(0, 1)
        load_w_codes(0, 0, 1)
        load_scales(x_planes, x_scales)
        load_scales(w_planes[0], w_scale_cols(0))
        load_w_codes(0, 1, 2)
        load_x_codes(1, 2)
        load_w_codes(0, 2, 4)
        load_x_codes(2, 4)
        nc.sync.dma_start(out=freqs[:], in_=freqs_cis.rearrange("(t p) j e -> p t j e", p=P))
        for c in range(1, len(CHUNKS)):
            load_scales(w_planes[c], w_scale_cols(c))
            load_w_codes(c, 0, 4)

        nc.scalar.copy(out=table_load[:], in_=zeros[:, 0:1])
        nc.gpsimd.tensor_copy(out=table[:, :, 0, :], in_=freqs[:, :, :, 0])
        nc.gpsimd.tensor_copy(out=table[:, :, 3, :], in_=freqs[:, :, :, 0])
        nc.gpsimd.tensor_copy(out=table[:, :, 2, :], in_=freqs[:, :, :, 1])
        nc.gpsimd.tensor_scalar(out=table[:, :, 1, :], in0=freqs[:, :, :, 1], scalar1=-1.0, scalar2=None, op0=MULT)

        warm = psum.tile([P, BLOCK], F32, name="acc")
        for i in range(WARM):
            nc.tensor.matmul(warm[:], lhsT=zeros[:, 0:P], rhs=zeros[:], start=True, stop=True)

        def chunk_of(block):
            for c in range(len(CHUNKS)):
                start, width = CHUNKS[c]
                if start <= block * BLOCK < start + width:
                    return c, block * BLOCK - start
            raise ValueError("block")

        def mx_pass(acc, m, block, g, first, width):
            c, at = chunk_of(block)
            a = at + first
            nc.tensor.matmul_mx(
                out=acc,
                lhsT=x_codes[:, g, 2 * P * m : 2 * P * (m + 1)].bitcast(FP4X4),
                lhsT_scale=x_planes[:, g, P * m : P * (m + 1)],
                rhs=w_codes[c][:, g, 2 * a : 2 * (a + width)].bitcast(FP4X4),
                rhs_scale=w_planes[c][:, g, a : a + width],
                start=(g == 0),
                stop=(g == PASSES - 1),
            )

        def rope_products(acc3, rope, m):
            n = len(range(rope, acc3.shape[1], 3))
            prod = prods.tile([P, 2, 3, 2, HALF], F32, name="prod")
            r = acc3[:, rope::3, :].rearrange("p r (h j) -> p r h j", h=2)
            t = table[:, m % 2, :, :].rearrange("p (c h) j -> p c h j", h=2)
            nc.vector.tensor_tensor(
                out=prod[:, :, 0:n, :, :].rearrange("p h r c j -> p r c h j"),
                in0=r.unsqueeze(2).to_broadcast([P, n, 2, 2, HALF]),
                in1=t.unsqueeze(1).to_broadcast([P, n, 2, 2, HALF]),
                op=MULT,
            )
            return prod, n

        def plain_copies(acc3, res3, rope):
            for r in range(3):
                if r != rope:
                    nc.scalar.copy(out=res3[:, r::3, :], in_=acc3[:, r::3, :])

        def rope_sum(res3, rope, prod, n):
            nc.vector.tensor_tensor(
                out=res3[:, rope::3, :],
                in0=prod[:, 0, 0:n, :, :].rearrange("p r c j -> p r (c j)"),
                in1=prod[:, 1, 0:n, :, :].rearrange("p r c j -> p r (c j)"),
                op=ADD,
            )

        def store(res, m, block, first, width):
            col = block * BLOCK + first
            nc.sync.dma_start(out=rows[P * m : P * (m + 1), col : col + width], in_=res[:, first : first + width])

        def units(tile_2d):
            return tile_2d.rearrange("p (u w) -> p u w", w=UNIT)

        waiting = []

        def finish():
            if waiting:
                res, m, block, rope, prod, n = waiting[0]
                rope_sum(units(res[:]), rope, prod, n)
                store(res, m, block, 0, BLOCK)
                waiting.clear()

        def direct_epilogue(acc, m, block):
            rope = (2 - 2 * block) % 3
            res = results.tile([P, BLOCK], F32, name="res")
            prod, n = rope_products(units(acc[:]), rope, m)
            plain_copies(units(acc[:]), units(res[:]), rope)
            finish()
            waiting.append((res, m, block, rope, prod, n))

        def epilogue(acc, m, block):
            rope = (2 - 2 * block) % 3
            res = results.tile([P, BLOCK], F32, name="res")
            nc.scalar.copy(out=res[:], in_=acc[:])
            finish()
            prod, n = rope_products(units(res[:]), rope, m)
            waiting.append((res, m, block, rope, prod, n))

        accs = []
        for m in range(TILES):
            acc = psum.tile([P, BLOCK], F32, name="acc")
            accs.append(acc)
        for g in range(PASSES):
            for m in range(TILES):
                mx_pass(accs[m][:], m, BLOCK_ORDER[0], g, 0, BLOCK)
        for m in range(TILES):
            epilogue(accs[m], m, BLOCK_ORDER[0])

        for block in BLOCK_ORDER[1:]:
            for m in range(TILES):
                if block == BLOCK_ORDER[-1] and m == TILES - 1:
                    continue
                acc = psum.tile([P, BLOCK], F32, name="acc")
                for g in range(PASSES):
                    mx_pass(acc[:], m, block, g, 0, BLOCK)
                if block == BLOCK_ORDER[-1]:
                    direct_epilogue(acc, m, block)
                else:
                    epilogue(acc, m, block)

        m, block = TILES - 1, BLOCK_ORDER[-1]
        res = results.tile([P, BLOCK], F32, name="res")
        acc_a = psum.tile([P, BLOCK], F32, name="acc")
        acc_b = psum.tile([P, BLOCK], F32, name="acc")
        acc_c = psum.tile([P, BLOCK], F32, name="acc")
        for acc, first, width in ((acc_a, 128, 256), (acc_b, 384, 128), (acc_c, 0, 128)):
            for g in range(PASSES):
                mx_pass(acc[:, 0:width], m, block, g, first, width)
        prod, n = rope_products(units(acc_a[:, 0:256]), 0, m)
        finish()
        rope_sum(units(res[:, 128:384]), 0, prod, n)
        nc.scalar.copy(out=res[:, 192:320], in_=acc_a[:, 64:192])
        nc.scalar.copy(out=res[:, 384:512], in_=acc_b[:, 0:128])
        store(res, m, block, 128, 384)
        nc.vector.tensor_copy(out=res[:, 0:128], in_=acc_c[:, 0:128])
        store(res, m, block, 0, 128)
